import numpy as np
import ml_dtypes


def mxq(x, axis, fmt="e4m3"):
    dtype, down = {"e4m3": (ml_dtypes.float8_e4m3fn, 7), "e5m2": (ml_dtypes.float8_e5m2, 14)}[fmt]
    v = np.moveaxis(np.asarray(x, np.float32).astype(ml_dtypes.bfloat16).astype(np.float64), axis, -1)
    blocks = v.reshape(v.shape[:-1] + (-1, 32))
    amax = np.abs(blocks).max(-1, keepdims=True)
    byte = np.maximum(np.where(amax > 0, np.frexp(amax)[1] - 1 + 127, 0) - down, 1)
    scale = np.exp2(byte - 127.0)
    codes = (blocks / scale).astype(np.float32).astype(dtype).astype(np.float64)
    return np.moveaxis((codes * scale).reshape(v.shape), -1, axis)


WIDE = False


def mx_kscale(k):
    if not WIDE:
        return np.ones(k)
    levels = np.array([10, -10, 5, -5, 0])
    if k % 512:
        return np.exp2(np.random.permutation(np.resize(levels, k // 32))).repeat(32)
    a = np.empty((k // 512, 16))
    for p in range(k // 512):
        a[p, :8] = np.random.permutation(np.resize(levels, 8))
        for g in range(8):
            far = levels[np.abs(levels - a[p, g]) >= 10]
            a[p, g + 8] = far[np.random.randint(len(far))]
    return np.exp2(a.ravel()).repeat(32)


BF16 = ml_dtypes.bfloat16


def bf(x):
    return np.asarray(x, np.float32).astype(BF16)


def f64(x):
    return np.asarray(x).astype(np.float64)


B, S, D, H, KV, HD = 2, 2048, 1024, 4, 2, 128
HALF = HD // 2
ROPE_BASE = 1.0e4


def rotate_half(t):
    return np.concatenate((-t[..., HALF:], t[..., :HALF]), axis=-1)


def setup_inputs():
    s = mx_kscale(D)
    inv_freq = 1.0 / ROPE_BASE ** (np.arange(HALF) / HALF)
    freqs = np.outer(np.arange(S), inv_freq)
    emb = np.concatenate((freqs, freqs), axis=-1)
    w = 1.0 / np.sqrt(D)
    return {"x": bf(np.random.standard_normal((B, S, D)) * s),
            "cos": bf(np.cos(emb)),
            "sin": bf(np.sin(emb)),
            "Wq": bf(np.random.standard_normal((D, H * HD)) * w / s[:, None]),
            "Wk": bf(np.random.standard_normal((D, KV * HD)) * w / s[:, None]),
            "Wv": bf(np.random.standard_normal((D, KV * HD)) * w / s[:, None])}


def reference(x, cos, sin, Wq, Wk, Wv):
    xq = mxq(f64(x), 2, "e4m3")
    q = (xq @ mxq(f64(Wq), 0, "e4m3")).reshape(B, S, H, HD)
    k = (xq @ mxq(f64(Wk), 0, "e4m3")).reshape(B, S, KV, HD)
    v = (xq @ mxq(f64(Wv), 0, "e4m3")).reshape(B, S, KV, HD)
    c = f64(cos)[None, :, None, :]
    sn = f64(sin)[None, :, None, :]
    q_rot = q * c + rotate_half(q) * sn
    k_rot = k * c + rotate_half(k) * sn
    return q_rot, k_rot, v

@@ -1,0 +1,223 @@
+from contextlib import ExitStack
+
+import concourse.mybir as mybir
+from concourse.masks import make_identity
+
+F32 = mybir.dt.float32
+BF16 = mybir.dt.bfloat16
+U32 = mybir.dt.uint32
+U8 = mybir.dt.uint8
+FP8X4 = mybir.dt.float8_e4m3fn_x4
+MULT = mybir.AluOpType.mult
+ADD = mybir.AluOpType.add
+
+P = 128
+B, S, D = 2, 2048, 1024
+HD = 128
+HALF = HD // 2
+Q_COLS, K_COLS, V_COLS = 512, 256, 256
+QK_COLS = Q_COLS + K_COLS
+N_COLS = QK_COLS + V_COLS
+K_PASS = 512
+PASSES = D // K_PASS
+PACK = 4
+SLOTS = 2
+BLOCK = P * SLOTS
+N_BLOCKS = B * S // BLOCK
+POS_BLOCKS = S // BLOCK
+WORDS = D // 2
+VECTOR_ADD_COLS = HD
+
+FLOPS = 2 * B * S * D * N_COLS
+
+
+def tile_attention_pa_t_kernel(tc, x, cos, sin, Wq, Wk, Wv, out_0, out_1, out_2):
+    nc = tc.nc
+    x_blocks = x.rearrange("b (p n s) k -> b n p (s k)", n=POS_BLOCKS, s=SLOTS)
+    q_blocks = out_0.rearrange("b (p n s) h d -> b n p (s h d)", n=POS_BLOCKS, s=SLOTS)
+    k_blocks = out_1.rearrange("b (p n s) h d -> b n p (s h d)", n=POS_BLOCKS, s=SLOTS)
+    v_blocks = out_2.rearrange("b (p n s) h d -> b n p (s h d)", n=POS_BLOCKS, s=SLOTS)
+
+    with ExitStack() as ctx:
+        keep = ctx.enter_context(tc.tile_pool(name="keep", bufs=1))
+        x_pool = ctx.enter_context(tc.tile_pool(name="x_pool", bufs=N_BLOCKS))
+        quant = ctx.enter_context(tc.tile_pool(name="quant", bufs=3))
+        result = ctx.enter_context(tc.tile_pool(name="result", bufs=6))
+        xt_psum = ctx.enter_context(tc.psum_pool(name="xt_psum", bufs=2))
+        acc_psum = ctx.enter_context(tc.psum_pool(name="acc_psum", bufs=6))
+
+        def load_weight(w, cols, name):
+            raw = keep.tile([P, PASSES * PACK, cols], BF16, name=name)
+            for c in range(PASSES):
+                nc.sync.dma_start(
+                    out=raw[:, c * PACK : (c + 1) * PACK, :],
+                    in_=w[c * K_PASS : (c + 1) * K_PASS, :].rearrange("(p t) n -> p t n", t=PACK),
+                )
+            return raw
+
+        def load_x(i):
+            x_blk = x_pool.tile([P, SLOTS * D], BF16)
+            nc.sync.dma_start(out=x_blk[:], in_=x_blocks[i // POS_BLOCKS, i % POS_BLOCKS])
+            return x_blk
+
+        wq_raw = load_weight(Wq, Q_COLS, "wq_raw")
+        wk_raw = load_weight(Wk, K_COLS, "wk_raw")
+        wv_raw = load_weight(Wv, V_COLS, "wv_raw")
+        x_tiles = [load_x(0), load_x(1)]
+        sin_raw = keep.tile([P, POS_BLOCKS, SLOTS, HD], BF16)
+        nc.sync.dma_start(
+            out=sin_raw[:].rearrange("p n s d -> p (n s d)"), in_=sin.rearrange("(p r) d -> p (r d)", p=P)
+        )
+        tables = keep.tile([P, POS_BLOCKS, 2, SLOTS, HD], BF16)
+        nc.sync.dma_start(
+            out=tables[:, :, 0, :, :].rearrange("p n s d -> p n (s d)"),
+            in_=cos.rearrange("(p n s) d -> p n (s d)", p=P, s=SLOTS),
+        )
+        for i in range(2, N_BLOCKS):
+            x_tiles.append(load_x(i))
+
+        ident = keep.tile([P, P], F32)
+        make_identity(nc, ident[:])
+
+        grouped_of = {}
+        codes_of = {}
+
+        def transpose_block(i):
+            x_words = x_tiles[i][:].bitcast(F32)
+            grouped = quant.tile([P, SLOTS * D], BF16, align_bytes=64)
+            grouped_words = grouped[:].bitcast(F32)
+            for s in range(SLOTS):
+                xt = xt_psum.tile([P, WORDS], F32)
+                for j in range(WORDS // P):
+                    c, u = divmod(j, 2)
+                    first = s * WORDS + c * 2 * P
+                    nc.tensor.transpose(
+                        xt[:, j * P : (j + 1) * P],
+                        x_words[:, first + u : first + 2 * P : 2],
+                        ident[:],
+                    )
+                nc.scalar.copy(
+                    out=grouped_words[:, s * WORDS : (s + 1) * WORDS].rearrange(
+                        "p (c r u) -> p c r u", c=PASSES, u=2
+                    ),
+                    in_=xt[:].rearrange("p (c u r) -> p c r u", c=PASSES, u=2),
+                )
+            grouped_of[i] = grouped
+
+        def quantise_block(i):
+            x_codes = quant.tile([P, SLOTS * PASSES * P], U32, align_bytes=64)
+            x_scales = quant.tile([P, SLOTS * PASSES * P], U8, align_bytes=64)
+            nc.vector.quantize_mx(
+                out=x_codes[:].bitcast(FP8X4), scales=x_scales[:], in_=grouped_of[i][:]
+            )
+            codes_of[i] = (x_codes, x_scales)
+
+        transpose_block(0)
+
+        w_grouped = keep.tile([P, PASSES, N_COLS, PACK], BF16, align_bytes=64)
+        w_codes = keep.tile([P, PASSES, N_COLS], U32, align_bytes=64)
+        w_scales = keep.tile([P, PASSES, N_COLS], U8, align_bytes=64)
+
+        def regroup_weight(copy, raw, first, cols):
+            for c in range(PASSES):
+                copy(
+                    out=w_grouped[:, c, first : first + cols, :].rearrange(
+                        "p (n i) t -> p n t i", i=4
+                    ),
+                    in_=raw[:, c * PACK : (c + 1) * PACK, :].rearrange("p t (n i) -> p n t i", i=4),
+                )
+
+        def quantise_weight(first, cols):
+            for c in range(PASSES):
+                nc.vector.quantize_mx(
+                    out=w_codes[:, c, first : first + cols].bitcast(FP8X4),
+                    scales=w_scales[:, c, first : first + cols],
+                    in_=w_grouped[:, c, first : first + cols, :].rearrange("p n t -> p (n t)"),
+                )
+
+        regroup_weight(nc.vector.tensor_copy, wq_raw, 0, Q_COLS)
+        regroup_weight(nc.vector.tensor_copy, wk_raw, Q_COLS, K_COLS)
+        regroup_weight(nc.scalar.copy, wv_raw, QK_COLS, V_COLS)
+        quantise_weight(0, Q_COLS)
+        quantise_weight(Q_COLS, K_COLS + V_COLS)
+        quantise_block(0)
+        nc.vector.tensor_copy(out=tables[:, :, 1, :, 0:HALF], in_=sin_raw[:, :, :, HALF:HD])
+        nc.vector.tensor_scalar_mul(
+            out=tables[:, :, 1, :, HALF:HD], in0=sin_raw[:, :, :, 0:HALF], scalar1=-1.0
+        )
+
+        banks_of = {}
+
+        def project(bank_cols, i, s, first, cols):
+            x_codes, x_scales = codes_of[i]
+            for c in range(PASSES):
+                tokens = slice((s * PASSES + c) * P, (s * PASSES + c + 1) * P)
+                nc.tensor.matmul_mx(
+                    out=bank_cols,
+                    lhsT=x_codes[:, tokens].bitcast(FP8X4),
+                    lhsT_scale=x_scales[:, tokens],
+                    rhs=w_codes[:, c, first : first + cols].bitcast(FP8X4),
+                    rhs_scale=w_scales[:, c, first : first + cols],
+                    start=(c == 0),
+                    stop=(c == PASSES - 1),
+                )
+
+        def project_block(i):
+            k_bank = acc_psum.tile([P, SLOTS * K_COLS], F32, tag="acc")
+            for s in range(SLOTS):
+                project(k_bank[:, s * K_COLS : (s + 1) * K_COLS], i, s, Q_COLS, K_COLS)
+            q_banks = []
+            for s in range(SLOTS):
+                q_bank = acc_psum.tile([P, Q_COLS], F32, tag="acc")
+                project(q_bank[:], i, s, 0, Q_COLS)
+                q_banks.append(q_bank)
+            v_bank = acc_psum.tile([P, SLOTS * V_COLS], F32, tag="acc")
+            for s in range(SLOTS):
+                project(v_bank[:, s * V_COLS : (s + 1) * V_COLS], i, s, QK_COLS, V_COLS)
+            banks_of[i] = (q_banks, k_bank, v_bank)
+
+        def rope_products(bank, n, first_slot, slots, products):
+            heads = bank.shape[1] // (slots * HD)
+            shape = [P, 2, slots, heads, HD]
+            nc.vector.tensor_tensor(
+                out=products.rearrange("p w (s h d) -> p w s h d", s=slots, d=HD),
+                in0=bank.rearrange("p (s h d) -> p s h d", s=slots, d=HD).unsqueeze(1).to_broadcast(shape),
+                in1=tables[:, n, :, first_slot : first_slot + slots, :].unsqueeze(3).to_broadcast(shape),
+                op=MULT,
+            )
+
+        def add_products(engine, both, cols):
+            by_cos = both[:, 0, cols].rearrange("p (g t j) -> p g t j", t=2, j=HALF)
+            by_sin = both[:, 1, cols].rearrange("p (g t j) -> p g t j", t=2, j=HALF)
+            engine.tensor_tensor(out=by_cos, in0=by_cos, in1=by_sin[:, :, ::-1, :], op=ADD)
+
+        def rope_block(i):
+            q_banks, k_bank, v_bank = banks_of[i]
+            n = i % POS_BLOCKS
+            both = result.tile([P, 2, SLOTS * QK_COLS], F32)
+            values = result.tile([P, SLOTS * V_COLS], F32)
+            nc.scalar.copy(out=values[:], in_=v_bank[:])
+            all_q = slice(0, SLOTS * Q_COLS)
+            all_k = slice(SLOTS * Q_COLS, SLOTS * QK_COLS)
+            rope_products(k_bank[:], n, 0, SLOTS, both[:, :, all_k])
+            for s in range(SLOTS):
+                rope_products(q_banks[s][:], n, s, 1, both[:, :, s * Q_COLS : (s + 1) * Q_COLS])
+            if i + 1 < N_BLOCKS:
+                add_products(nc.vector, both, slice(SLOTS * QK_COLS - VECTOR_ADD_COLS, SLOTS * QK_COLS))
+                add_products(nc.gpsimd, both, slice(0, SLOTS * QK_COLS - VECTOR_ADD_COLS))
+            else:
+                add_products(nc.gpsimd, both, all_k)
+                add_products(nc.vector, both, all_q)
+            rot = both[:, 0, :]
+            b = i // POS_BLOCKS
+            nc.sync.dma_start(out=v_blocks[b, n], in_=values[:])
+            nc.sync.dma_start(out=k_blocks[b, n], in_=rot[:, all_k])
+            nc.sync.dma_start(out=q_blocks[b, n], in_=rot[:, all_q])
+
+        for i in range(N_BLOCKS):
+            if i + 1 < N_BLOCKS:
+                transpose_block(i + 1)
+            project_block(i)
+            if i + 1 < N_BLOCKS:
+                quantise_block(i + 1)
+            rope_block(i)

@@ -17,7 +17,6 @@ HD = 128
 HALF = HD // 2
 Q_COLS, K_COLS, V_COLS = 512, 256, 256
 QK_COLS = Q_COLS + K_COLS
-N_COLS = QK_COLS + V_COLS
 K_PASS = 512
 PASSES = D // K_PASS
 PACK = 4
@@ -26,9 +25,10 @@ BLOCK = P * SLOTS
 N_BLOCKS = B * S // BLOCK
 POS_BLOCKS = S // BLOCK
 WORDS = D // 2
+EARLY = 2
 VECTOR_ADD_COLS = HD
 
-FLOPS = 2 * B * S * D * N_COLS
+FLOPS = 2 * B * S * D * (QK_COLS + V_COLS)
 
 
 def tile_attention_pa_t_kernel(tc, x, cos, sin, Wq, Wk, Wv, out_0, out_1, out_2):
@@ -37,47 +37,86 @@ def tile_attention_pa_t_kernel(tc, x, cos, sin, Wq, Wk, Wv, out_0, out_1, out_2)
     q_blocks = out_0.rearrange("b (p n s) h d -> b n p (s h d)", n=POS_BLOCKS, s=SLOTS)
     k_blocks = out_1.rearrange("b (p n s) h d -> b n p (s h d)", n=POS_BLOCKS, s=SLOTS)
     v_blocks = out_2.rearrange("b (p n s) h d -> b n p (s h d)", n=POS_BLOCKS, s=SLOTS)
+    cos_rows = cos.rearrange("(p n s) d -> p n (s d)", p=P, s=SLOTS)
+    sin_rows = sin.rearrange("(p n s) d -> p n (s d)", p=P, s=SLOTS)
 
     with ExitStack() as ctx:
         keep = ctx.enter_context(tc.tile_pool(name="keep", bufs=1))
         x_pool = ctx.enter_context(tc.tile_pool(name="x_pool", bufs=N_BLOCKS))
-        quant = ctx.enter_context(tc.tile_pool(name="quant", bufs=3))
-        result = ctx.enter_context(tc.tile_pool(name="result", bufs=6))
+        quant = ctx.enter_context(tc.tile_pool(name="quant", bufs=4))
+        result = ctx.enter_context(tc.tile_pool(name="result", bufs=5))
         xt_psum = ctx.enter_context(tc.psum_pool(name="xt_psum", bufs=2))
         acc_psum = ctx.enter_context(tc.psum_pool(name="acc_psum", bufs=6))
 
-        def load_weight(w, cols, name):
-            raw = keep.tile([P, PASSES * PACK, cols], BF16, name=name)
-            for c in range(PASSES):
-                nc.sync.dma_start(
-                    out=raw[:, c * PACK : (c + 1) * PACK, :],
-                    in_=w[c * K_PASS : (c + 1) * K_PASS, :].rearrange("(p t) n -> p t n", t=PACK),
-                )
-            return raw
-
-        def load_x(i):
-            x_blk = x_pool.tile([P, SLOTS * D], BF16)
-            nc.sync.dma_start(out=x_blk[:], in_=x_blocks[i // POS_BLOCKS, i % POS_BLOCKS])
-            return x_blk
-
-        wq_raw = load_weight(Wq, Q_COLS, "wq_raw")
-        wk_raw = load_weight(Wk, K_COLS, "wk_raw")
-        wv_raw = load_weight(Wv, V_COLS, "wv_raw")
-        x_tiles = [load_x(0), load_x(1)]
-        sin_raw = keep.tile([P, POS_BLOCKS, SLOTS, HD], BF16)
-        nc.sync.dma_start(
-            out=sin_raw[:].rearrange("p n s d -> p (n s d)"), in_=sin.rearrange("(p r) d -> p (r d)", p=P)
-        )
-        tables = keep.tile([P, POS_BLOCKS, 2, SLOTS, HD], BF16)
-        nc.sync.dma_start(
-            out=tables[:, :, 0, :, :].rearrange("p n s d -> p n (s d)"),
-            in_=cos.rearrange("(p n s) d -> p n (s d)", p=P, s=SLOTS),
-        )
-        for i in range(2, N_BLOCKS):
-            x_tiles.append(load_x(i))
-
         ident = keep.tile([P, P], F32)
         make_identity(nc, ident[:])
+
+        ctx.enter_context(tc.manual_schedule())
+
+        def weight_tiles(cols, name):
+            raw = keep.tile([P, PASSES * PACK, cols], BF16, name=name + "_raw")
+            grouped = keep.tile([P, PASSES, cols, PACK], BF16, name=name + "_grouped", align_bytes=64)
+            codes = keep.tile([P, PASSES, cols], U32, name=name + "_codes", align_bytes=64)
+            scales = keep.tile([P, PASSES, cols], U8, name=name + "_scales", align_bytes=64)
+            return raw, grouped, codes, scales
+
+        def load_weight(weight, w):
+            for c in range(PASSES):
+                nc.sync.dma_start(
+                    out=weight[0][:, c * PACK : (c + 1) * PACK, :],
+                    in_=w[c * K_PASS : (c + 1) * K_PASS, :].rearrange("(p t) n -> p t n", t=PACK),
+                )
+
+        x_tiles = []
+
+        def load_x(pieces):
+            i = len(x_tiles)
+            x_blk = x_pool.tile([P, SLOTS * D], BF16)
+            width = SLOTS * D // pieces
+            for j in range(pieces):
+                part = slice(j * width, (j + 1) * width)
+                nc.sync.dma_start(out=x_blk[:, part], in_=x_blocks[i // POS_BLOCKS, i % POS_BLOCKS][:, part])
+            x_tiles.append(x_blk)
+
+        sin_raw = keep.tile([P, POS_BLOCKS, SLOTS, HD], BF16)
+        tables = keep.tile([P, POS_BLOCKS, 2, SLOTS, HD], BF16)
+
+        def load_tables(blocks):
+            nc.sync.dma_start(
+                out=tables[:, blocks, 0, :, :].rearrange("p n s d -> p n (s d)"), in_=cos_rows[:, blocks, :]
+            )
+            nc.sync.dma_start(
+                out=sin_raw[:, blocks, :, :].rearrange("p n s d -> p n (s d)"), in_=sin_rows[:, blocks, :]
+            )
+
+        wq, wk, wv = weight_tiles(Q_COLS, "wq"), weight_tiles(K_COLS, "wk"), weight_tiles(V_COLS, "wv")
+        load_weight(wk, Wk)
+        load_x(SLOTS)
+        load_tables(slice(0, EARLY))
+        load_weight(wq, Wq)
+        load_weight(wv, Wv)
+        load_x(1)
+        load_x(1)
+        load_tables(slice(EARLY, POS_BLOCKS))
+        for i in range(3, N_BLOCKS):
+            load_x(1)
+
+        def gpsimd_copy(out, in_):
+            nc.gpsimd.tensor_scalar(out=out, in0=in_, scalar1=1.0, scalar2=0.0, op0=MULT, op1=ADD)
+
+        def regroup_weight(copy, weight, c, cols):
+            copy(
+                out=weight[1][:, c, cols, :].rearrange("p (n i) t -> p n t i", i=4),
+                in_=weight[0][:, c * PACK : (c + 1) * PACK, cols].rearrange("p t (n i) -> p n t i", i=4),
+            )
+
+        def quantise_weight(weight, passes):
+            grouped, codes, scales = weight[1:]
+            nc.vector.quantize_mx(
+                out=codes[:, passes, :].rearrange("p c n -> p (c n)").bitcast(FP8X4),
+                scales=scales[:, passes, :].rearrange("p c n -> p (c n)"),
+                in_=grouped[:, passes, :, :].rearrange("p c n t -> p (c n t)"),
+            )
 
         grouped_of = {}
         codes_of = {}
@@ -102,53 +141,23 @@ def tile_attention_pa_t_kernel(tc, x, cos, sin, Wq, Wk, Wv, out_0, out_1, out_2)
                     ),
                     in_=xt[:].rearrange("p (c u r) -> p c r u", c=PASSES, u=2),
                 )
-            grouped_of[i] = grouped
-
-        def quantise_block(i):
             x_codes = quant.tile([P, SLOTS * PASSES * P], U32, align_bytes=64)
             x_scales = quant.tile([P, SLOTS * PASSES * P], U8, align_bytes=64)
-            nc.vector.quantize_mx(
-                out=x_codes[:].bitcast(FP8X4), scales=x_scales[:], in_=grouped_of[i][:]
-            )
+            grouped_of[i] = grouped
             codes_of[i] = (x_codes, x_scales)
 
-        transpose_block(0)
-
-        w_grouped = keep.tile([P, PASSES, N_COLS, PACK], BF16, align_bytes=64)
-        w_codes = keep.tile([P, PASSES, N_COLS], U32, align_bytes=64)
-        w_scales = keep.tile([P, PASSES, N_COLS], U8, align_bytes=64)
-
-        def regroup_weight(copy, raw, first, cols):
-            for c in range(PASSES):
-                copy(
-                    out=w_grouped[:, c, first : first + cols, :].rearrange(
-                        "p (n i) t -> p n t i", i=4
-                    ),
-                    in_=raw[:, c * PACK : (c + 1) * PACK, :].rearrange("p t (n i) -> p n t i", i=4),
-                )
-
-        def quantise_weight(first, cols):
-            for c in range(PASSES):
+        def quantise_block(i, pieces):
+            x_codes, x_scales = codes_of[i]
+            words = SLOTS * PASSES * P // pieces
+            for j in range(pieces):
+                part = slice(j * words, (j + 1) * words)
                 nc.vector.quantize_mx(
-                    out=w_codes[:, c, first : first + cols].bitcast(FP8X4),
-                    scales=w_scales[:, c, first : first + cols],
-                    in_=w_grouped[:, c, first : first + cols, :].rearrange("p n t -> p (n t)"),
+                    out=x_codes[:, part].bitcast(FP8X4),
+                    scales=x_scales[:, part],
+                    in_=grouped_of[i][:, j * words * PACK : (j + 1) * words * PACK],
                 )
 
-        regroup_weight(nc.vector.tensor_copy, wq_raw, 0, Q_COLS)
-        regroup_weight(nc.vector.tensor_copy, wk_raw, Q_COLS, K_COLS)
-        regroup_weight(nc.scalar.copy, wv_raw, QK_COLS, V_COLS)
-        quantise_weight(0, Q_COLS)
-        quantise_weight(Q_COLS, K_COLS + V_COLS)
-        quantise_block(0)
-        nc.vector.tensor_copy(out=tables[:, :, 1, :, 0:HALF], in_=sin_raw[:, :, :, HALF:HD])
-        nc.vector.tensor_scalar_mul(
-            out=tables[:, :, 1, :, HALF:HD], in0=sin_raw[:, :, :, 0:HALF], scalar1=-1.0
-        )
-
-        banks_of = {}
-
-        def project(bank_cols, i, s, first, cols):
+        def project(bank_cols, i, s, weight):
             x_codes, x_scales = codes_of[i]
             for c in range(PASSES):
                 tokens = slice((s * PASSES + c) * P, (s * PASSES + c + 1) * P)
@@ -156,68 +165,126 @@ def tile_attention_pa_t_kernel(tc, x, cos, sin, Wq, Wk, Wv, out_0, out_1, out_2)
                     out=bank_cols,
                     lhsT=x_codes[:, tokens].bitcast(FP8X4),
                     lhsT_scale=x_scales[:, tokens],
-                    rhs=w_codes[:, c, first : first + cols].bitcast(FP8X4),
-                    rhs_scale=w_scales[:, c, first : first + cols],
+                    rhs=weight[2][:, c, :].bitcast(FP8X4),
+                    rhs_scale=weight[3][:, c, :],
                     start=(c == 0),
                     stop=(c == PASSES - 1),
                 )
 
-        def project_block(i):
-            k_bank = acc_psum.tile([P, SLOTS * K_COLS], F32, tag="acc")
+        def project_both(i, weight, cols):
+            bank = acc_psum.tile([P, SLOTS * cols], F32, tag="acc")
             for s in range(SLOTS):
-                project(k_bank[:, s * K_COLS : (s + 1) * K_COLS], i, s, Q_COLS, K_COLS)
-            q_banks = []
-            for s in range(SLOTS):
-                q_bank = acc_psum.tile([P, Q_COLS], F32, tag="acc")
-                project(q_bank[:], i, s, 0, Q_COLS)
-                q_banks.append(q_bank)
-            v_bank = acc_psum.tile([P, SLOTS * V_COLS], F32, tag="acc")
-            for s in range(SLOTS):
-                project(v_bank[:, s * V_COLS : (s + 1) * V_COLS], i, s, QK_COLS, V_COLS)
-            banks_of[i] = (q_banks, k_bank, v_bank)
+                project(bank[:, s * cols : (s + 1) * cols], i, s, weight)
+            return bank
 
-        def rope_products(bank, n, first_slot, slots, products):
-            heads = bank.shape[1] // (slots * HD)
-            shape = [P, 2, slots, heads, HD]
+        def project_queries(i):
+            banks = []
+            for s in range(SLOTS):
+                bank = acc_psum.tile([P, Q_COLS], F32, tag="acc")
+                project(bank[:], i, s, wq)
+                banks.append(bank)
+            return banks
+
+        both_of = {}
+
+        def rope_products(bank, i, first_slot, slots, first_col):
+            cols = bank.shape[1]
+            shape = [P, 2, slots, cols // (slots * HD), HD]
             nc.vector.tensor_tensor(
-                out=products.rearrange("p w (s h d) -> p w s h d", s=slots, d=HD),
+                out=both_of[i][:, :, first_col : first_col + cols].rearrange("p w (s h d) -> p w s h d", s=slots, d=HD),
                 in0=bank.rearrange("p (s h d) -> p s h d", s=slots, d=HD).unsqueeze(1).to_broadcast(shape),
-                in1=tables[:, n, :, first_slot : first_slot + slots, :].unsqueeze(3).to_broadcast(shape),
+                in1=tables[:, i % POS_BLOCKS, :, first_slot : first_slot + slots, :].unsqueeze(3).to_broadcast(shape),
                 op=MULT,
             )
 
-        def add_products(engine, both, cols):
-            by_cos = both[:, 0, cols].rearrange("p (g t j) -> p g t j", t=2, j=HALF)
-            by_sin = both[:, 1, cols].rearrange("p (g t j) -> p g t j", t=2, j=HALF)
+        def add_products(engine, i, first, end):
+            by_cos = both_of[i][:, 0, first:end].rearrange("p (g t j) -> p g t j", t=2, j=HALF)
+            by_sin = both_of[i][:, 1, first:end].rearrange("p (g t j) -> p g t j", t=2, j=HALF)
             engine.tensor_tensor(out=by_cos, in0=by_cos, in1=by_sin[:, :, ::-1, :], op=ADD)
 
-        def rope_block(i):
-            q_banks, k_bank, v_bank = banks_of[i]
-            n = i % POS_BLOCKS
-            both = result.tile([P, 2, SLOTS * QK_COLS], F32)
+        def build_tables(copy, negate, blocks):
+            copy(out=tables[:, blocks, 1, :, 0:HALF], in_=sin_raw[:, blocks, :, HALF:HD])
+            negate(tables[:, blocks, 1, :, HALF:HD], sin_raw[:, blocks, :, 0:HALF])
+
+        def gpsimd_negate(out, in_):
+            nc.gpsimd.tensor_scalar(out=out, in0=in_, scalar1=-1.0, scalar2=0.0, op0=MULT, op1=ADD)
+
+        def scalar_negate(out, in_):
+            nc.scalar.mul(out, in_, -1.0)
+
+        QUERIES = SLOTS * Q_COLS
+        ALL = SLOTS * QK_COLS
+
+        def store_values(i, bank):
             values = result.tile([P, SLOTS * V_COLS], F32)
-            nc.scalar.copy(out=values[:], in_=v_bank[:])
-            all_q = slice(0, SLOTS * Q_COLS)
-            all_k = slice(SLOTS * Q_COLS, SLOTS * QK_COLS)
-            rope_products(k_bank[:], n, 0, SLOTS, both[:, :, all_k])
-            for s in range(SLOTS):
-                rope_products(q_banks[s][:], n, s, 1, both[:, :, s * Q_COLS : (s + 1) * Q_COLS])
-            if i + 1 < N_BLOCKS:
-                add_products(nc.vector, both, slice(SLOTS * QK_COLS - VECTOR_ADD_COLS, SLOTS * QK_COLS))
-                add_products(nc.gpsimd, both, slice(0, SLOTS * QK_COLS - VECTOR_ADD_COLS))
-            else:
-                add_products(nc.gpsimd, both, all_k)
-                add_products(nc.vector, both, all_q)
-            rot = both[:, 0, :]
-            b = i // POS_BLOCKS
-            nc.sync.dma_start(out=v_blocks[b, n], in_=values[:])
-            nc.sync.dma_start(out=k_blocks[b, n], in_=rot[:, all_k])
-            nc.sync.dma_start(out=q_blocks[b, n], in_=rot[:, all_q])
+            nc.scalar.copy(out=values[:], in_=bank[:])
+            nc.sync.dma_start(out=v_blocks[i // POS_BLOCKS, i % POS_BLOCKS], in_=values[:])
+
+        def store_keys(i):
+            nc.sync.dma_start(out=k_blocks[i // POS_BLOCKS, i % POS_BLOCKS], in_=both_of[i][:, 0, QUERIES:ALL])
+
+        def store_queries(i, first, end):
+            nc.sync.dma_start(
+                out=q_blocks[i // POS_BLOCKS, i % POS_BLOCKS][:, first:end], in_=both_of[i][:, 0, first:end]
+            )
+
+        for c in range(PASSES):
+            regroup_weight(nc.vector.tensor_copy, wk, c, slice(0, K_COLS))
+        quantise_weight(wk, slice(0, PASSES))
+        transpose_block(0)
+        build_tables(gpsimd_copy, gpsimd_negate, slice(0, EARLY))
+        quantise_block(0, SLOTS)
+        def regroup_queries(c):
+            regroup_weight(nc.vector.tensor_copy, wq, c, slice(0, 2 * HD))
+            regroup_weight(nc.scalar.copy, wq, c, slice(2 * HD, 3 * HD))
+            regroup_weight(gpsimd_copy, wq, c, slice(3 * HD, 4 * HD))
+
+        regroup_queries(0)
 
         for i in range(N_BLOCKS):
-            if i + 1 < N_BLOCKS:
-                transpose_block(i + 1)
-            project_block(i)
-            if i + 1 < N_BLOCKS:
-                quantise_block(i + 1)
-            rope_block(i)
+            last = i == N_BLOCKS - 1
+            both_of[i] = result.tile([P, 2, ALL], F32, name="both")
+            if not last:
+                k_bank = project_both(i, wk, K_COLS)
+                rope_products(k_bank[:], i, 0, SLOTS, QUERIES)
+            if i == 0:
+                regroup_queries(1)
+                for c in range(PASSES):
+                    quantise_weight(wq, slice(c, c + 1))
+                    regroup_weight(nc.scalar.copy, wv, c, slice(0, V_COLS))
+            if i == 1:
+                quantise_block(2, 1)
+            if 0 < i and i + 2 < N_BLOCKS:
+                transpose_block(i + 2)
+            q_banks = project_queries(i)
+            if i == 0:
+                transpose_block(1)
+                transpose_block(2)
+            rope_products(q_banks[0][:], i, 0, 1, 0)
+            if i == 0:
+                quantise_weight(wv, slice(0, PASSES))
+                quantise_block(1, 1)
+                build_tables(nc.scalar.copy, scalar_negate, slice(EARLY, POS_BLOCKS))
+            if last:
+                rope_products(q_banks[1][:], i, 1, 1, Q_COLS)
+                k_bank = project_both(i, wk, K_COLS)
+                rope_products(k_bank[:], i, 0, SLOTS, QUERIES)
+            else:
+                most = Q_COLS - HD
+                rope_products(q_banks[1][:, 0:most], i, 1, 1, Q_COLS)
+                add_products(nc.vector, i, ALL - VECTOR_ADD_COLS, ALL)
+                if 0 < i and i + 2 < N_BLOCKS:
+                    quantise_block(i + 2, 1)
+                rope_products(q_banks[1][:, most:Q_COLS], i, 1, 1, Q_COLS + most)
+                add_products(nc.gpsimd, i, 0, ALL - VECTOR_ADD_COLS)
+            v_bank = project_both(i, wv, V_COLS)
+            store_values(i, v_bank)
+            if i > 0:
+                store_keys(i - 1)
+                store_queries(i - 1, 0, QUERIES)
+        i = N_BLOCKS - 1
+        for s in range(SLOTS):
+            add_products(nc.vector, i, s * Q_COLS, (s + 1) * Q_COLS)
+            store_queries(i, s * Q_COLS, (s + 1) * Q_COLS)
+        add_products(nc.vector, i, QUERIES, ALL)
+        store_keys(i)

@@ -26,7 +26,7 @@ N_BLOCKS = B * S // BLOCK
 POS_BLOCKS = S // BLOCK
 WORDS = D // 2
 EARLY = 2
-VECTOR_ADD_COLS = HD
+VECTOR_ADD_COLS = 3 * HD
 
 FLOPS = 2 * B * S * D * (QK_COLS + V_COLS)
 

@@ -26,7 +26,8 @@ N_BLOCKS = B * S // BLOCK
 POS_BLOCKS = S // BLOCK
 WORDS = D // 2
 EARLY = 2
-VECTOR_ADD_COLS = 3 * HD
+VECTOR_ADD_COLS = K_COLS
+LOADED_AHEAD = 9
 
 FLOPS = 2 * B * S * D * (QK_COLS + V_COLS)
 
@@ -43,7 +44,7 @@ def tile_attention_pa_t_kernel(tc, x, cos, sin, Wq, Wk, Wv, out_0, out_1, out_2)
     with ExitStack() as ctx:
         keep = ctx.enter_context(tc.tile_pool(name="keep", bufs=1))
         x_pool = ctx.enter_context(tc.tile_pool(name="x_pool", bufs=N_BLOCKS))
-        quant = ctx.enter_context(tc.tile_pool(name="quant", bufs=4))
+        quant = ctx.enter_context(tc.tile_pool(name="quant", bufs=5))
         result = ctx.enter_context(tc.tile_pool(name="result", bufs=5))
         xt_psum = ctx.enter_context(tc.psum_pool(name="xt_psum", bufs=2))
         acc_psum = ctx.enter_context(tc.psum_pool(name="acc_psum", bufs=6))
@@ -94,15 +95,12 @@ def tile_attention_pa_t_kernel(tc, x, cos, sin, Wq, Wk, Wv, out_0, out_1, out_2)
         load_x(SLOTS)
         load_tables(slice(0, EARLY))
         load_weight(wq, Wq)
+        load_x(1)
         load_weight(wv, Wv)
         load_x(1)
-        load_x(1)
         load_tables(slice(EARLY, POS_BLOCKS))
-        for i in range(3, N_BLOCKS):
+        while len(x_tiles) < LOADED_AHEAD:
             load_x(1)
-
-        def gpsimd_copy(out, in_):
-            nc.gpsimd.tensor_scalar(out=out, in0=in_, scalar1=1.0, scalar2=0.0, op0=MULT, op1=ADD)
 
         def regroup_weight(copy, weight, c, cols):
             copy(
@@ -206,8 +204,8 @@ def tile_attention_pa_t_kernel(tc, x, cos, sin, Wq, Wk, Wv, out_0, out_1, out_2)
             copy(out=tables[:, blocks, 1, :, 0:HALF], in_=sin_raw[:, blocks, :, HALF:HD])
             negate(tables[:, blocks, 1, :, HALF:HD], sin_raw[:, blocks, :, 0:HALF])
 
-        def gpsimd_negate(out, in_):
-            nc.gpsimd.tensor_scalar(out=out, in0=in_, scalar1=-1.0, scalar2=0.0, op0=MULT, op1=ADD)
+        def vector_negate(out, in_):
+            nc.vector.tensor_scalar_mul(out=out, in0=in_, scalar1=-1.0)
 
         def scalar_negate(out, in_):
             nc.scalar.mul(out, in_, -1.0)
@@ -228,61 +226,88 @@ def tile_attention_pa_t_kernel(tc, x, cos, sin, Wq, Wk, Wv, out_0, out_1, out_2)
                 out=q_blocks[i // POS_BLOCKS, i % POS_BLOCKS][:, first:end], in_=both_of[i][:, 0, first:end]
             )
 
+        def store_block(i):
+            store_queries(i, 0, QUERIES)
+            store_keys(i)
+
+        def vector_adds(i):
+            add_products(nc.vector, i, ALL - VECTOR_ADD_COLS, ALL)
+
+        def gpsimd_adds(i):
+            add_products(nc.gpsimd, i, 0, ALL - VECTOR_ADD_COLS)
+
         for c in range(PASSES):
             regroup_weight(nc.vector.tensor_copy, wk, c, slice(0, K_COLS))
         quantise_weight(wk, slice(0, PASSES))
+        build_tables(nc.vector.tensor_copy, vector_negate, slice(0, EARLY))
         transpose_block(0)
-        build_tables(gpsimd_copy, gpsimd_negate, slice(0, EARLY))
         quantise_block(0, SLOTS)
-        def regroup_queries(c):
-            regroup_weight(nc.vector.tensor_copy, wq, c, slice(0, 2 * HD))
-            regroup_weight(nc.scalar.copy, wq, c, slice(2 * HD, 3 * HD))
-            regroup_weight(gpsimd_copy, wq, c, slice(3 * HD, 4 * HD))
+        first_half, second_half = slice(0, Q_COLS // 2), slice(Q_COLS // 2, Q_COLS)
+        regroup_weight(nc.vector.tensor_copy, wq, 0, first_half)
+        k_banks = {0: project_both(0, wk, K_COLS)}
+        regroup_weight(nc.scalar.copy, wq, 0, second_half)
+        regroup_weight(nc.scalar.copy, wq, 1, second_half)
+        for c in range(PASSES):
+            regroup_weight(nc.scalar.copy, wv, c, slice(0, V_COLS))
 
-        regroup_queries(0)
+        def keys(i):
+            rope_products(k_banks[i][:], i, 0, SLOTS, QUERIES)
 
+        def queries(i, banks, s, first, end):
+            rope_products(banks[s][:, first:end], i, s, 1, s * Q_COLS + first)
+
+        SPLIT = Q_COLS - HD
         for i in range(N_BLOCKS):
             last = i == N_BLOCKS - 1
             both_of[i] = result.tile([P, 2, ALL], F32, name="both")
             if not last:
-                k_bank = project_both(i, wk, K_COLS)
-                rope_products(k_bank[:], i, 0, SLOTS, QUERIES)
+                keys(i)
             if i == 0:
-                regroup_queries(1)
+                regroup_weight(nc.vector.tensor_copy, wq, 1, first_half)
+                transpose_block(1)
                 for c in range(PASSES):
                     quantise_weight(wq, slice(c, c + 1))
-                    regroup_weight(nc.scalar.copy, wv, c, slice(0, V_COLS))
-            if i == 1:
-                quantise_block(2, 1)
-            if 0 < i and i + 2 < N_BLOCKS:
-                transpose_block(i + 2)
-            q_banks = project_queries(i)
-            if i == 0:
-                transpose_block(1)
-                transpose_block(2)
-            rope_products(q_banks[0][:], i, 0, 1, 0)
-            if i == 0:
                 quantise_weight(wv, slice(0, PASSES))
+            q_banks = project_queries(i)
+            queries(i, q_banks, 0, 0, Q_COLS)
+            if i == 0:
+                transpose_block(2)
                 quantise_block(1, 1)
                 build_tables(nc.scalar.copy, scalar_negate, slice(EARLY, POS_BLOCKS))
-            if last:
-                rope_products(q_banks[1][:], i, 1, 1, Q_COLS)
-                k_bank = project_both(i, wk, K_COLS)
-                rope_products(k_bank[:], i, 0, SLOTS, QUERIES)
-            else:
-                most = Q_COLS - HD
-                rope_products(q_banks[1][:, 0:most], i, 1, 1, Q_COLS)
-                add_products(nc.vector, i, ALL - VECTOR_ADD_COLS, ALL)
-                if 0 < i and i + 2 < N_BLOCKS:
-                    quantise_block(i + 2, 1)
-                rope_products(q_banks[1][:, most:Q_COLS], i, 1, 1, Q_COLS + most)
-                add_products(nc.gpsimd, i, 0, ALL - VECTOR_ADD_COLS)
-            v_bank = project_both(i, wv, V_COLS)
-            store_values(i, v_bank)
+            elif i % 2 == 1:
+                for j in (i + 2, i + 3):
+                    if j < N_BLOCKS:
+                        transpose_block(j)
+            if not last:
+                k_banks[i + 1] = project_both(i + 1, wk, K_COLS)
             if i > 0:
-                store_keys(i - 1)
-                store_queries(i - 1, 0, QUERIES)
+                v_bank = project_both(i - 1, wv, V_COLS)
+                store_values(i - 1, v_bank)
+            if last:
+                queries(i, q_banks, 1, 0, Q_COLS)
+                keys(i)
+            elif i % 2 == 0:
+                queries(i, q_banks, 1, 0, Q_COLS)
+                gpsimd_adds(i)
+                if i == 0:
+                    quantise_block(2, 1)
+            else:
+                queries(i, q_banks, 1, 0, SPLIT)
+                vector_adds(i - 1)
+                vector_adds(i)
+                for j in (i + 2, i + 3):
+                    if j < N_BLOCKS:
+                        quantise_block(j, 1)
+                queries(i, q_banks, 1, SPLIT, Q_COLS)
+                gpsimd_adds(i)
+            if len(x_tiles) < N_BLOCKS:
+                load_x(1)
+            if 0 < i and not last:
+                store_block(i - 1)
         i = N_BLOCKS - 1
+        store_values(i, project_both(i, wv, V_COLS))
+        vector_adds(i - 1)
+        store_block(i - 1)
         for s in range(SLOTS):
             add_products(nc.vector, i, s * Q_COLS, (s + 1) * Q_COLS)
             store_queries(i, s * Q_COLS, (s + 1) * Q_COLS)

@@ -26,8 +26,10 @@ N_BLOCKS = B * S // BLOCK
 POS_BLOCKS = S // BLOCK
 WORDS = D // 2
 EARLY = 2
-VECTOR_ADD_COLS = K_COLS
 LOADED_AHEAD = 9
+QUANTISED_AFTER = {1: (3, 4), 3: (5, 6, 7), 6: (8, 9, 10, 11), 10: (12, 13, 14, 15), 13: ()}
+TRANSPOSED_IN = {1: (3, 4), 2: (5, 6), 3: (7,), 4: (8,), 5: (9, 10), 6: (11,), 7: (12,), 8: (13,), 9: (14,), 10: (15,)}
+VALUES_LAG = 3
 
 FLOPS = 2 * B * S * D * (QK_COLS + V_COLS)
 
@@ -43,9 +45,9 @@ def tile_attention_pa_t_kernel(tc, x, cos, sin, Wq, Wk, Wv, out_0, out_1, out_2)
 
     with ExitStack() as ctx:
         keep = ctx.enter_context(tc.tile_pool(name="keep", bufs=1))
-        x_pool = ctx.enter_context(tc.tile_pool(name="x_pool", bufs=N_BLOCKS))
-        quant = ctx.enter_context(tc.tile_pool(name="quant", bufs=5))
-        result = ctx.enter_context(tc.tile_pool(name="result", bufs=5))
+        x_pool = ctx.enter_context(tc.tile_pool(name="x_pool", bufs=LOADED_AHEAD + 2))
+        quant = ctx.enter_context(tc.tile_pool(name="quant", bufs=9))
+        result = ctx.enter_context(tc.tile_pool(name="result", bufs=6))
         xt_psum = ctx.enter_context(tc.psum_pool(name="xt_psum", bufs=2))
         acc_psum = ctx.enter_context(tc.psum_pool(name="acc_psum", bufs=6))
 
@@ -91,8 +93,8 @@ def tile_attention_pa_t_kernel(tc, x, cos, sin, Wq, Wk, Wv, out_0, out_1, out_2)
             )
 
         wq, wk, wv = weight_tiles(Q_COLS, "wq"), weight_tiles(K_COLS, "wk"), weight_tiles(V_COLS, "wv")
-        load_weight(wk, Wk)
         load_x(SLOTS)
+        load_weight(wk, Wk)
         load_tables(slice(0, EARLY))
         load_weight(wq, Wq)
         load_x(1)
@@ -121,7 +123,7 @@ def tile_attention_pa_t_kernel(tc, x, cos, sin, Wq, Wk, Wv, out_0, out_1, out_2)
 
         def transpose_block(i):
             x_words = x_tiles[i][:].bitcast(F32)
-            grouped = quant.tile([P, SLOTS * D], BF16, align_bytes=64)
+            grouped = quant.tile([P, SLOTS * D], BF16, align_bytes=64, bufs=6)
             grouped_words = grouped[:].bitcast(F32)
             for s in range(SLOTS):
                 xt = xt_psum.tile([P, WORDS], F32)
@@ -214,7 +216,7 @@ def tile_attention_pa_t_kernel(tc, x, cos, sin, Wq, Wk, Wv, out_0, out_1, out_2)
         ALL = SLOTS * QK_COLS
 
         def store_values(i, bank):
-            values = result.tile([P, SLOTS * V_COLS], F32)
+            values = result.tile([P, SLOTS * V_COLS], F32, bufs=4)
             nc.scalar.copy(out=values[:], in_=bank[:])
             nc.sync.dma_start(out=v_blocks[i // POS_BLOCKS, i % POS_BLOCKS], in_=values[:])
 
@@ -226,29 +228,27 @@ def tile_attention_pa_t_kernel(tc, x, cos, sin, Wq, Wk, Wv, out_0, out_1, out_2)
                 out=q_blocks[i // POS_BLOCKS, i % POS_BLOCKS][:, first:end], in_=both_of[i][:, 0, first:end]
             )
 
-        def store_block(i):
-            store_queries(i, 0, QUERIES)
-            store_keys(i)
+        def vector_heads(i):
+            return 0 if i == 0 else 1 + i % 2
 
         def vector_adds(i):
-            add_products(nc.vector, i, ALL - VECTOR_ADD_COLS, ALL)
+            if vector_heads(i):
+                add_products(nc.vector, i, ALL - vector_heads(i) * HD, ALL)
 
         def gpsimd_adds(i):
-            add_products(nc.gpsimd, i, 0, ALL - VECTOR_ADD_COLS)
+            add_products(nc.gpsimd, i, 0, ALL - vector_heads(i) * HD)
 
+        transpose_block(0)
         for c in range(PASSES):
             regroup_weight(nc.vector.tensor_copy, wk, c, slice(0, K_COLS))
+        quantise_block(0, SLOTS)
         quantise_weight(wk, slice(0, PASSES))
         build_tables(nc.vector.tensor_copy, vector_negate, slice(0, EARLY))
-        transpose_block(0)
-        quantise_block(0, SLOTS)
         first_half, second_half = slice(0, Q_COLS // 2), slice(Q_COLS // 2, Q_COLS)
         regroup_weight(nc.vector.tensor_copy, wq, 0, first_half)
         k_banks = {0: project_both(0, wk, K_COLS)}
         regroup_weight(nc.scalar.copy, wq, 0, second_half)
-        regroup_weight(nc.scalar.copy, wq, 1, second_half)
-        for c in range(PASSES):
-            regroup_weight(nc.scalar.copy, wv, c, slice(0, V_COLS))
+        regroup_weight(nc.scalar.copy, wq, 1, slice(0, Q_COLS))
 
         def keys(i):
             rope_products(k_banks[i][:], i, 0, SLOTS, QUERIES)
@@ -257,57 +257,66 @@ def tile_attention_pa_t_kernel(tc, x, cos, sin, Wq, Wk, Wv, out_0, out_1, out_2)
             rope_products(banks[s][:, first:end], i, s, 1, s * Q_COLS + first)
 
         SPLIT = Q_COLS - HD
+        added = 0
+        stored = 0
+        projected = 0
         for i in range(N_BLOCKS):
             last = i == N_BLOCKS - 1
             both_of[i] = result.tile([P, 2, ALL], F32, name="both")
             if not last:
                 keys(i)
             if i == 0:
-                regroup_weight(nc.vector.tensor_copy, wq, 1, first_half)
                 transpose_block(1)
                 for c in range(PASSES):
                     quantise_weight(wq, slice(c, c + 1))
-                quantise_weight(wv, slice(0, PASSES))
+                quantise_block(1, 1)
+                for c in range(PASSES):
+                    regroup_weight(nc.scalar.copy, wv, c, slice(0, V_COLS))
             q_banks = project_queries(i)
             queries(i, q_banks, 0, 0, Q_COLS)
             if i == 0:
                 transpose_block(2)
-                quantise_block(1, 1)
+                quantise_weight(wv, slice(0, PASSES))
                 build_tables(nc.scalar.copy, scalar_negate, slice(EARLY, POS_BLOCKS))
-            elif i % 2 == 1:
-                for j in (i + 2, i + 3):
-                    if j < N_BLOCKS:
-                        transpose_block(j)
+            for j in TRANSPOSED_IN.get(i, ()):
+                transpose_block(j)
             if not last:
                 k_banks[i + 1] = project_both(i + 1, wk, K_COLS)
-            if i > 0:
-                v_bank = project_both(i - 1, wv, V_COLS)
-                store_values(i - 1, v_bank)
+            lag = VALUES_LAG if i + 1 in TRANSPOSED_IN or i in TRANSPOSED_IN else 1
+            for j in range(projected, min(i - lag + 1, projected + 2)):
+                store_values(j, project_both(j, wv, V_COLS))
+                projected = j + 1
             if last:
                 queries(i, q_banks, 1, 0, Q_COLS)
                 keys(i)
-            elif i % 2 == 0:
+            elif i in QUANTISED_AFTER:
+                queries(i, q_banks, 1, 0, SPLIT)
+                for j in range(added, i + 1):
+                    vector_adds(j)
+                added = i + 1
+                for j in QUANTISED_AFTER[i]:
+                    quantise_block(j, 1)
+                queries(i, q_banks, 1, SPLIT, Q_COLS)
+                gpsimd_adds(i)
+            else:
                 queries(i, q_banks, 1, 0, Q_COLS)
                 gpsimd_adds(i)
                 if i == 0:
                     quantise_block(2, 1)
-            else:
-                queries(i, q_banks, 1, 0, SPLIT)
-                vector_adds(i - 1)
-                vector_adds(i)
-                for j in (i + 2, i + 3):
-                    if j < N_BLOCKS:
-                        quantise_block(j, 1)
-                queries(i, q_banks, 1, SPLIT, Q_COLS)
-                gpsimd_adds(i)
             if len(x_tiles) < N_BLOCKS:
                 load_x(1)
             if 0 < i and not last:
-                store_block(i - 1)
+                store_queries(i - 1, 0, QUERIES)
+                for j in range(stored, min(added, i)):
+                    store_keys(j)
+                    stored = j + 1
         i = N_BLOCKS - 1
         store_values(i, project_both(i, wv, V_COLS))
-        vector_adds(i - 1)
-        store_block(i - 1)
+        store_queries(i - 1, 0, QUERIES)
+        for j in range(added, i):
+            vector_adds(j)
+        for j in range(stored, i):
+            store_keys(j)
         for s in range(SLOTS):
             add_products(nc.vector, i, s * Q_COLS, (s + 1) * Q_COLS)
             store_queries(i, s * Q_COLS, (s + 1) * Q_COLS)

@@ -27,9 +27,10 @@ POS_BLOCKS = S // BLOCK
 WORDS = D // 2
 EARLY = 2
 LOADED_AHEAD = 9
-QUANTISED_AFTER = {1: (3, 4), 3: (5, 6, 7), 6: (8, 9, 10, 11), 10: (12, 13, 14, 15), 13: ()}
-TRANSPOSED_IN = {1: (3, 4), 2: (5, 6), 3: (7,), 4: (8,), 5: (9, 10), 6: (11,), 7: (12,), 8: (13,), 9: (14,), 10: (15,)}
-VALUES_LAG = 3
+QUANTISED_AFTER = {0: (2, 3), 2: (4, 5), 4: (6, 7, 8), 7: (9, 10, 11, 12), 11: (13, 14, 15)}
+TRANSPOSED_IN = {1: (4,), 2: (5,), 3: (6, 7), 4: (8,), 5: (9, 10), 6: (11,), 7: (12,), 8: (13,), 9: (14,), 10: (15,)}
+TENSOR_ADDS_FROM = 10
+VALUES_LAG = 2
 
 FLOPS = 2 * B * S * D * (QK_COLS + V_COLS)
 
@@ -72,13 +73,10 @@ def tile_attention_pa_t_kernel(tc, x, cos, sin, Wq, Wk, Wv, out_0, out_1, out_2)
 
         x_tiles = []
 
-        def load_x(pieces):
+        def load_x():
             i = len(x_tiles)
             x_blk = x_pool.tile([P, SLOTS * D], BF16)
-            width = SLOTS * D // pieces
-            for j in range(pieces):
-                part = slice(j * width, (j + 1) * width)
-                nc.sync.dma_start(out=x_blk[:, part], in_=x_blocks[i // POS_BLOCKS, i % POS_BLOCKS][:, part])
+            nc.sync.dma_start(out=x_blk[:], in_=x_blocks[i // POS_BLOCKS, i % POS_BLOCKS])
             x_tiles.append(x_blk)
 
         sin_raw = keep.tile([P, POS_BLOCKS, SLOTS, HD], BF16)
@@ -93,16 +91,20 @@ def tile_attention_pa_t_kernel(tc, x, cos, sin, Wq, Wk, Wv, out_0, out_1, out_2)
             )
 
         wq, wk, wv = weight_tiles(Q_COLS, "wq"), weight_tiles(K_COLS, "wk"), weight_tiles(V_COLS, "wv")
-        load_x(SLOTS)
+        x_first = x_pool.tile([P, SLOTS * D], BF16, name="x_blk")
+        nc.sync.dma_start(out=x_first[:, 0:D], in_=x_blocks[0, 0][:, 0:D])
         load_weight(wk, Wk)
+        nc.sync.dma_start(out=x_first[:, D : SLOTS * D], in_=x_blocks[0, 0][:, D : SLOTS * D])
+        x_tiles.append(x_first)
         load_tables(slice(0, EARLY))
+        load_x()
         load_weight(wq, Wq)
-        load_x(1)
+        load_x()
         load_weight(wv, Wv)
-        load_x(1)
+        load_x()
         load_tables(slice(EARLY, POS_BLOCKS))
         while len(x_tiles) < LOADED_AHEAD:
-            load_x(1)
+            load_x()
 
         def regroup_weight(copy, weight, c, cols):
             copy(
@@ -146,16 +148,14 @@ def tile_attention_pa_t_kernel(tc, x, cos, sin, Wq, Wk, Wv, out_0, out_1, out_2)
             grouped_of[i] = grouped
             codes_of[i] = (x_codes, x_scales)
 
-        def quantise_block(i, pieces):
+        def quantise_block(i, first_slot, slots):
             x_codes, x_scales = codes_of[i]
-            words = SLOTS * PASSES * P // pieces
-            for j in range(pieces):
-                part = slice(j * words, (j + 1) * words)
-                nc.vector.quantize_mx(
-                    out=x_codes[:, part].bitcast(FP8X4),
-                    scales=x_scales[:, part],
-                    in_=grouped_of[i][:, j * words * PACK : (j + 1) * words * PACK],
-                )
+            first, end = first_slot * PASSES * P, (first_slot + slots) * PASSES * P
+            nc.vector.quantize_mx(
+                out=x_codes[:, first:end].bitcast(FP8X4),
+                scales=x_scales[:, first:end],
+                in_=grouped_of[i][:, first * PACK : end * PACK],
+            )
 
         def project(bank_cols, i, s, weight):
             x_codes, x_scales = codes_of[i]
@@ -228,27 +228,31 @@ def tile_attention_pa_t_kernel(tc, x, cos, sin, Wq, Wk, Wv, out_0, out_1, out_2)
                 out=q_blocks[i // POS_BLOCKS, i % POS_BLOCKS][:, first:end], in_=both_of[i][:, 0, first:end]
             )
 
-        def vector_heads(i):
-            return 0 if i == 0 else 1 + i % 2
+        def shared_heads(i):
+            return 0 if i < 2 else 2 if i >= TENSOR_ADDS_FROM else 2 - i % 2
 
         def vector_adds(i):
-            if vector_heads(i):
-                add_products(nc.vector, i, ALL - vector_heads(i) * HD, ALL)
+            if shared_heads(i):
+                add_products(nc.vector, i, ALL - shared_heads(i) * HD, ALL)
+
+        def tensor_adds(i):
+            cols = shared_heads(i) * HD
+            bank = acc_psum.tile([P, cols], F32, tag="acc")
+            sums = bank[:].rearrange("p (g t j) -> p g t j", t=2, j=HALF)
+            by_cos = both_of[i][:, 0, ALL - cols : ALL].rearrange("p (g t j) -> p g t j", t=2, j=HALF)
+            by_sin = both_of[i][:, 1, ALL - cols : ALL].rearrange("p (g t j) -> p g t j", t=2, j=HALF)
+            for t in range(2):
+                nc.tensor.matmul(out=sums[:, :, t, :], lhsT=ident[:], rhs=by_cos[:, :, t, :], start=True, stop=False)
+                nc.tensor.matmul(out=sums[:, :, t, :], lhsT=ident[:], rhs=by_sin[:, :, 1 - t, :], start=False, stop=True)
+            nc.scalar.copy(out=both_of[i][:, 0, ALL - cols : ALL], in_=bank[:])
 
         def gpsimd_adds(i):
-            add_products(nc.gpsimd, i, 0, ALL - vector_heads(i) * HD)
+            add_products(nc.gpsimd, i, 0, QUERIES if i < 2 else ALL - shared_heads(i) * HD)
 
-        transpose_block(0)
-        for c in range(PASSES):
-            regroup_weight(nc.vector.tensor_copy, wk, c, slice(0, K_COLS))
-        quantise_block(0, SLOTS)
-        quantise_weight(wk, slice(0, PASSES))
-        build_tables(nc.vector.tensor_copy, vector_negate, slice(0, EARLY))
-        first_half, second_half = slice(0, Q_COLS // 2), slice(Q_COLS // 2, Q_COLS)
-        regroup_weight(nc.vector.tensor_copy, wq, 0, first_half)
-        k_banks = {0: project_both(0, wk, K_COLS)}
-        regroup_weight(nc.scalar.copy, wq, 0, second_half)
-        regroup_weight(nc.scalar.copy, wq, 1, slice(0, Q_COLS))
+        def new_block(i):
+            both_of[i] = result.tile([P, 2, ALL], F32, name="both")
+
+        k_banks = {}
 
         def keys(i):
             rope_products(k_banks[i][:], i, 0, SLOTS, QUERIES)
@@ -256,32 +260,57 @@ def tile_attention_pa_t_kernel(tc, x, cos, sin, Wq, Wk, Wv, out_0, out_1, out_2)
         def queries(i, banks, s, first, end):
             rope_products(banks[s][:, first:end], i, s, 1, s * Q_COLS + first)
 
+        new_block(0)
+        transpose_block(0)
+        for c in range(PASSES):
+            regroup_weight(nc.vector.tensor_copy, wk, c, slice(0, K_COLS))
+        quantise_block(0, 0, 1)
+        quantise_weight(wk, slice(0, PASSES))
+        build_tables(nc.vector.tensor_copy, vector_negate, slice(0, EARLY))
+        quantise_block(0, 1, 1)
+        for s in range(SLOTS):
+            bank = acc_psum.tile([P, K_COLS], F32, tag="acc")
+            project(bank[:], 0, s, wk)
+            rope_products(bank[:], 0, s, 1, QUERIES + s * K_COLS)
+        new_block(1)
+        first_half, second_half = slice(0, Q_COLS // 2), slice(Q_COLS // 2, Q_COLS)
+        regroup_weight(nc.scalar.copy, wq, 0, second_half)
+        transpose_block(1)
+        regroup_weight(nc.scalar.copy, wq, 1, second_half)
+        for c in range(PASSES):
+            regroup_weight(nc.vector.tensor_copy, wq, c, first_half)
+        quantise_block(1, 0, SLOTS)
+        k_banks[1] = project_both(1, wk, K_COLS)
+        regroup_weight(nc.scalar.copy, wv, 0, slice(0, V_COLS))
+        transpose_block(2)
+        regroup_weight(nc.scalar.copy, wv, 1, slice(0, V_COLS))
+        for c in range(PASSES):
+            quantise_weight(wq, slice(c, c + 1))
+        keys(1)
+        for j in range(2):
+            add_products(nc.gpsimd, j, QUERIES, ALL)
+
         SPLIT = Q_COLS - HD
         added = 0
         stored = 0
         projected = 0
         for i in range(N_BLOCKS):
             last = i == N_BLOCKS - 1
-            both_of[i] = result.tile([P, 2, ALL], F32, name="both")
-            if not last:
-                keys(i)
-            if i == 0:
-                transpose_block(1)
-                for c in range(PASSES):
-                    quantise_weight(wq, slice(c, c + 1))
-                quantise_block(1, 1)
-                for c in range(PASSES):
-                    regroup_weight(nc.scalar.copy, wv, c, slice(0, V_COLS))
+            if i > 1:
+                new_block(i)
+                if not last:
+                    keys(i)
             q_banks = project_queries(i)
             queries(i, q_banks, 0, 0, Q_COLS)
             if i == 0:
-                transpose_block(2)
-                quantise_weight(wv, slice(0, PASSES))
+                transpose_block(3)
                 build_tables(nc.scalar.copy, scalar_negate, slice(EARLY, POS_BLOCKS))
             for j in TRANSPOSED_IN.get(i, ()):
                 transpose_block(j)
-            if not last:
+            if 0 < i and not last:
                 k_banks[i + 1] = project_both(i + 1, wk, K_COLS)
+            if i > TENSOR_ADDS_FROM:
+                tensor_adds(i - 1)
             lag = VALUES_LAG if i + 1 in TRANSPOSED_IN or i in TRANSPOSED_IN else 1
             for j in range(projected, min(i - lag + 1, projected + 2)):
                 store_values(j, project_both(j, wv, V_COLS))
@@ -291,20 +320,22 @@ def tile_attention_pa_t_kernel(tc, x, cos, sin, Wq, Wk, Wv, out_0, out_1, out_2)
                 keys(i)
             elif i in QUANTISED_AFTER:
                 queries(i, q_banks, 1, 0, SPLIT)
-                for j in range(added, i + 1):
+                if i == 0:
+                    quantise_weight(wv, slice(0, PASSES))
+                for j in range(added, min(i + 1, TENSOR_ADDS_FROM)):
                     vector_adds(j)
-                added = i + 1
+                    added = j + 1
                 for j in QUANTISED_AFTER[i]:
-                    quantise_block(j, 1)
+                    quantise_block(j, 0, SLOTS)
                 queries(i, q_banks, 1, SPLIT, Q_COLS)
                 gpsimd_adds(i)
             else:
                 queries(i, q_banks, 1, 0, Q_COLS)
                 gpsimd_adds(i)
-                if i == 0:
-                    quantise_block(2, 1)
+            if i > TENSOR_ADDS_FROM:
+                added = i
             if len(x_tiles) < N_BLOCKS:
-                load_x(1)
+                load_x()
             if 0 < i and not last:
                 store_queries(i - 1, 0, QUERIES)
                 for j in range(stored, min(added, i)):
@@ -313,12 +344,9 @@ def tile_attention_pa_t_kernel(tc, x, cos, sin, Wq, Wk, Wv, out_0, out_1, out_2)
         i = N_BLOCKS - 1
         store_values(i, project_both(i, wv, V_COLS))
         store_queries(i - 1, 0, QUERIES)
-        for j in range(added, i):
-            vector_adds(j)
-        for j in range(stored, i):
-            store_keys(j)
-        for s in range(SLOTS):
-            add_products(nc.vector, i, s * Q_COLS, (s + 1) * Q_COLS)
+        store_keys(i - 1)
+        for s, engine in ((1, nc.vector), (0, nc.gpsimd)):
+            add_products(engine, i, s * Q_COLS, (s + 1) * Q_COLS)
             store_queries(i, s * Q_COLS, (s + 1) * Q_COLS)
         add_products(nc.vector, i, QUERIES, ALL)
         store_keys(i)

@@ -229,6 +229,8 @@ def tile_attention_pa_t_kernel(tc, x, cos, sin, Wq, Wk, Wv, out_0, out_1, out_2)
             )
 
         def shared_heads(i):
+            if i == N_BLOCKS - 1:
+                return SLOTS * K_COLS // HD
             return 0 if i < 2 else 2 if i >= TENSOR_ADDS_FROM else 2 - i % 2
 
         def vector_adds(i):
@@ -298,8 +300,7 @@ def tile_attention_pa_t_kernel(tc, x, cos, sin, Wq, Wk, Wv, out_0, out_1, out_2)
             last = i == N_BLOCKS - 1
             if i > 1:
                 new_block(i)
-                if not last:
-                    keys(i)
+                keys(i)
             q_banks = project_queries(i)
             queries(i, q_banks, 0, 0, Q_COLS)
             if i == 0:
@@ -307,17 +308,16 @@ def tile_attention_pa_t_kernel(tc, x, cos, sin, Wq, Wk, Wv, out_0, out_1, out_2)
                 build_tables(nc.scalar.copy, scalar_negate, slice(EARLY, POS_BLOCKS))
             for j in TRANSPOSED_IN.get(i, ()):
                 transpose_block(j)
-            if 0 < i and not last:
+            if 0 < i < N_BLOCKS - 1:
                 k_banks[i + 1] = project_both(i + 1, wk, K_COLS)
             if i > TENSOR_ADDS_FROM:
                 tensor_adds(i - 1)
             lag = VALUES_LAG if i + 1 in TRANSPOSED_IN or i in TRANSPOSED_IN else 1
-            for j in range(projected, min(i - lag + 1, projected + 2)):
+            for j in range(projected, N_BLOCKS if last else min(i - lag + 1, projected + 2)):
                 store_values(j, project_both(j, wv, V_COLS))
                 projected = j + 1
             if last:
                 queries(i, q_banks, 1, 0, Q_COLS)
-                keys(i)
             elif i in QUANTISED_AFTER:
                 queries(i, q_banks, 1, 0, SPLIT)
                 if i == 0:
@@ -342,11 +342,11 @@ def tile_attention_pa_t_kernel(tc, x, cos, sin, Wq, Wk, Wv, out_0, out_1, out_2)
                     store_keys(j)
                     stored = j + 1
         i = N_BLOCKS - 1
-        store_values(i, project_both(i, wv, V_COLS))
+        tensor_adds(i)
         store_queries(i - 1, 0, QUERIES)
         store_keys(i - 1)
-        for s, engine in ((1, nc.vector), (0, nc.gpsimd)):
-            add_products(engine, i, s * Q_COLS, (s + 1) * Q_COLS)
-            store_queries(i, s * Q_COLS, (s + 1) * Q_COLS)
-        add_products(nc.vector, i, QUERIES, ALL)
-        store_keys(i)
+        for first, end in ((0, Q_COLS), (Q_COLS, QUERIES - HD), (QUERIES - HD, QUERIES)):
+            add_products(nc.vector, i, first, end)
+            store_queries(i, first, end)
+            if first == 0:
+                store_keys(i)

@@ -26,10 +26,10 @@ N_BLOCKS = B * S // BLOCK
 POS_BLOCKS = S // BLOCK
 WORDS = D // 2
 EARLY = 2
-LOADED_AHEAD = 9
 QUANTISED_AFTER = {0: (2, 3), 2: (4, 5), 4: (6, 7, 8), 7: (9, 10, 11, 12), 11: (13, 14, 15)}
 TRANSPOSED_IN = {1: (4,), 2: (5,), 3: (6, 7), 4: (8,), 5: (9, 10), 6: (11,), 7: (12,), 8: (13,), 9: (14,), 10: (15,)}
 TENSOR_ADDS_FROM = 10
+SORTED_FROM = 6
 VALUES_LAG = 2
 
 FLOPS = 2 * B * S * D * (QK_COLS + V_COLS)
@@ -46,9 +46,9 @@ def tile_attention_pa_t_kernel(tc, x, cos, sin, Wq, Wk, Wv, out_0, out_1, out_2)
 
     with ExitStack() as ctx:
         keep = ctx.enter_context(tc.tile_pool(name="keep", bufs=1))
-        x_pool = ctx.enter_context(tc.tile_pool(name="x_pool", bufs=LOADED_AHEAD + 2))
-        quant = ctx.enter_context(tc.tile_pool(name="quant", bufs=9))
-        result = ctx.enter_context(tc.tile_pool(name="result", bufs=6))
+        x_pool = ctx.enter_context(tc.tile_pool(name="x_pool", bufs=N_BLOCKS))
+        quant = ctx.enter_context(tc.tile_pool(name="quant", bufs=8))
+        result = ctx.enter_context(tc.tile_pool(name="result", bufs=5))
         xt_psum = ctx.enter_context(tc.psum_pool(name="xt_psum", bufs=2))
         acc_psum = ctx.enter_context(tc.psum_pool(name="acc_psum", bufs=6))
 
@@ -58,17 +58,22 @@ def tile_attention_pa_t_kernel(tc, x, cos, sin, Wq, Wk, Wv, out_0, out_1, out_2)
         ctx.enter_context(tc.manual_schedule())
 
         def weight_tiles(cols, name):
-            raw = keep.tile([P, PASSES * PACK, cols], BF16, name=name + "_raw")
+            raw = []
             grouped = keep.tile([P, PASSES, cols, PACK], BF16, name=name + "_grouped", align_bytes=64)
             codes = keep.tile([P, PASSES, cols], U32, name=name + "_codes", align_bytes=64)
             scales = keep.tile([P, PASSES, cols], U8, name=name + "_scales", align_bytes=64)
             return raw, grouped, codes, scales
 
         def load_weight(weight, w):
+            cols = w.shape[1]
             for c in range(PASSES):
+                if c * PACK * cols % (SLOTS * D) == 0:
+                    raw = x_pool.tile([P, SLOTS * D], BF16, name="x_blk")
+                first = c * PACK * cols % (SLOTS * D)
+                part = raw[:, first : first + PACK * cols].rearrange("p (t n) -> p t n", t=PACK)
+                weight[0].append(part)
                 nc.sync.dma_start(
-                    out=weight[0][:, c * PACK : (c + 1) * PACK, :],
-                    in_=w[c * K_PASS : (c + 1) * K_PASS, :].rearrange("(p t) n -> p t n", t=PACK),
+                    out=part, in_=w[c * K_PASS : (c + 1) * K_PASS, :].rearrange("(p t) n -> p t n", t=PACK)
                 )
 
         x_tiles = []
@@ -103,13 +108,13 @@ def tile_attention_pa_t_kernel(tc, x, cos, sin, Wq, Wk, Wv, out_0, out_1, out_2)
         load_weight(wv, Wv)
         load_x()
         load_tables(slice(EARLY, POS_BLOCKS))
-        while len(x_tiles) < LOADED_AHEAD:
+        while len(x_tiles) < N_BLOCKS:
             load_x()
 
         def regroup_weight(copy, weight, c, cols):
             copy(
                 out=weight[1][:, c, cols, :].rearrange("p (n i) t -> p n t i", i=4),
-                in_=weight[0][:, c * PACK : (c + 1) * PACK, cols].rearrange("p t (n i) -> p n t i", i=4),
+                in_=weight[0][c][:, :, cols].rearrange("p t (n i) -> p n t i", i=4),
             )
 
         def quantise_weight(weight, passes):
@@ -123,6 +128,16 @@ def tile_attention_pa_t_kernel(tc, x, cos, sin, Wq, Wk, Wv, out_0, out_1, out_2)
         grouped_of = {}
         codes_of = {}
 
+        sorted_of = {}
+
+        def sort_words(i):
+            x_sorted = quant.tile([P, SLOTS * WORDS], F32, bufs=4)
+            nc.scalar.copy(
+                out=x_sorted[:].rearrange("p (g u r) -> p g u r", u=2, r=P),
+                in_=x_tiles[i][:].bitcast(F32).rearrange("p (g r u) -> p g u r", u=2, r=P),
+            )
+            sorted_of[i] = x_sorted
+
         def transpose_block(i):
             x_words = x_tiles[i][:].bitcast(F32)
             grouped = quant.tile([P, SLOTS * D], BF16, align_bytes=64, bufs=6)
@@ -132,11 +147,11 @@ def tile_attention_pa_t_kernel(tc, x, cos, sin, Wq, Wk, Wv, out_0, out_1, out_2)
                 for j in range(WORDS // P):
                     c, u = divmod(j, 2)
                     first = s * WORDS + c * 2 * P
-                    nc.tensor.transpose(
-                        xt[:, j * P : (j + 1) * P],
-                        x_words[:, first + u : first + 2 * P : 2],
-                        ident[:],
-                    )
+                    if i < SORTED_FROM:
+                        words = x_words[:, first + u : first + 2 * P : 2]
+                    else:
+                        words = sorted_of[i][:, first + u * P : first + (u + 1) * P]
+                    nc.tensor.transpose(xt[:, j * P : (j + 1) * P], words, ident[:])
                 nc.scalar.copy(
                     out=grouped_words[:, s * WORDS : (s + 1) * WORDS].rearrange(
                         "p (c r u) -> p c r u", c=PASSES, u=2
@@ -308,6 +323,9 @@ def tile_attention_pa_t_kernel(tc, x, cos, sin, Wq, Wk, Wv, out_0, out_1, out_2)
                 build_tables(nc.scalar.copy, scalar_negate, slice(EARLY, POS_BLOCKS))
             for j in TRANSPOSED_IN.get(i, ()):
                 transpose_block(j)
+            for j in TRANSPOSED_IN.get(i + 2, ()):
+                if j >= SORTED_FROM:
+                    sort_words(j)
             if 0 < i < N_BLOCKS - 1:
                 k_banks[i + 1] = project_both(i + 1, wk, K_COLS)
             if i > TENSOR_ADDS_FROM:
@@ -334,8 +352,6 @@ def tile_attention_pa_t_kernel(tc, x, cos, sin, Wq, Wk, Wv, out_0, out_1, out_2)
                 gpsimd_adds(i)
             if i > TENSOR_ADDS_FROM:
                 added = i
-            if len(x_tiles) < N_BLOCKS:
-                load_x()
             if 0 < i and not last:
                 store_queries(i - 1, 0, QUERIES)
                 for j in range(stored, min(added, i)):

@@ -277,8 +277,18 @@ def tile_attention_pa_t_kernel(tc, x, cos, sin, Wq, Wk, Wv, out_0, out_1, out_2)
         def queries(i, banks, s, first, end):
             rope_products(banks[s][:, first:end], i, s, 1, s * Q_COLS + first)
 
+        zeros = keep.tile([P, Q_COLS], BF16)
+        nc.vector.memset(zeros[:], 0.0)
+
+        def warm_up(products):
+            bank = acc_psum.tile([P, Q_COLS], F32, tag="acc")
+            for j in range(products):
+                nc.tensor.matmul(out=bank[:], lhsT=zeros[:, 0:P], rhs=zeros[:], start=True, stop=True)
+
         new_block(0)
+        warm_up(4)
         transpose_block(0)
+        warm_up(2)
         for c in range(PASSES):
             regroup_weight(nc.vector.tensor_copy, wk, c, slice(0, K_COLS))
         quantise_block(0, 0, 1)
@@ -293,6 +303,7 @@ def tile_attention_pa_t_kernel(tc, x, cos, sin, Wq, Wk, Wv, out_0, out_1, out_2)
         first_half, second_half = slice(0, Q_COLS // 2), slice(Q_COLS // 2, Q_COLS)
         regroup_weight(nc.scalar.copy, wq, 0, second_half)
         transpose_block(1)
+        warm_up(6)
         regroup_weight(nc.scalar.copy, wq, 1, second_half)
         for c in range(PASSES):
             regroup_weight(nc.vector.tensor_copy, wq, c, first_half)

@@ -30,7 +30,6 @@ QUANTISED_AFTER = {0: (2, 3), 2: (4, 5), 4: (6, 7, 8), 7: (9, 10, 11, 12), 11: (
 TRANSPOSED_IN = {1: (4,), 2: (5,), 3: (6, 7), 4: (8,), 5: (9, 10), 6: (11,), 7: (12,), 8: (13,), 9: (14,), 10: (15,)}
 TENSOR_ADDS_FROM = 10
 SORTED_FROM = 6
-VALUES_LAG = 2
 
 FLOPS = 2 * B * S * D * (QK_COLS + V_COLS)
 
@@ -245,7 +244,7 @@ def tile_attention_pa_t_kernel(tc, x, cos, sin, Wq, Wk, Wv, out_0, out_1, out_2)
 
         def shared_heads(i):
             if i == N_BLOCKS - 1:
-                return SLOTS * K_COLS // HD
+                return SLOTS * K_COLS // HD - 1
             return 0 if i < 2 else 2 if i >= TENSOR_ADDS_FROM else 2 - i % 2
 
         def vector_adds(i):
@@ -295,19 +294,20 @@ def tile_attention_pa_t_kernel(tc, x, cos, sin, Wq, Wk, Wv, out_0, out_1, out_2)
         quantise_weight(wk, slice(0, PASSES))
         build_tables(nc.vector.tensor_copy, vector_negate, slice(0, EARLY))
         quantise_block(0, 1, 1)
+        first_half, second_half = slice(0, Q_COLS // 2), slice(Q_COLS // 2, Q_COLS)
+        new_block(1)
         for s in range(SLOTS):
             bank = acc_psum.tile([P, K_COLS], F32, tag="acc")
             project(bank[:], 0, s, wk)
             rope_products(bank[:], 0, s, 1, QUERIES + s * K_COLS)
-        new_block(1)
-        first_half, second_half = slice(0, Q_COLS // 2), slice(Q_COLS // 2, Q_COLS)
-        regroup_weight(nc.scalar.copy, wq, 0, second_half)
-        transpose_block(1)
+            if s == 0:
+                transpose_block(1)
+                regroup_weight(nc.vector.tensor_copy, wq, 0, first_half)
         warm_up(6)
-        regroup_weight(nc.scalar.copy, wq, 1, second_half)
         for c in range(PASSES):
-            regroup_weight(nc.vector.tensor_copy, wq, c, first_half)
+            regroup_weight(nc.scalar.copy, wq, c, second_half)
         quantise_block(1, 0, SLOTS)
+        regroup_weight(nc.vector.tensor_copy, wq, 1, first_half)
         k_banks[1] = project_both(1, wk, K_COLS)
         regroup_weight(nc.scalar.copy, wv, 0, slice(0, V_COLS))
         transpose_block(2)
@@ -341,10 +341,9 @@ def tile_attention_pa_t_kernel(tc, x, cos, sin, Wq, Wk, Wv, out_0, out_1, out_2)
                 k_banks[i + 1] = project_both(i + 1, wk, K_COLS)
             if i > TENSOR_ADDS_FROM:
                 tensor_adds(i - 1)
-            lag = VALUES_LAG if i + 1 in TRANSPOSED_IN or i in TRANSPOSED_IN else 1
-            for j in range(projected, N_BLOCKS if last else min(i - lag + 1, projected + 2)):
-                store_values(j, project_both(j, wv, V_COLS))
-                projected = j + 1
+            while projected < min(N_BLOCKS, i - 1 + sum(2 < j <= i for j in QUANTISED_AFTER)):
+                store_values(projected, project_both(projected, wv, V_COLS))
+                projected += 1
             if last:
                 queries(i, q_banks, 1, 0, Q_COLS)
             elif i in QUANTISED_AFTER:
@@ -372,8 +371,10 @@ def tile_attention_pa_t_kernel(tc, x, cos, sin, Wq, Wk, Wv, out_0, out_1, out_2)
         tensor_adds(i)
         store_queries(i - 1, 0, QUERIES)
         store_keys(i - 1)
-        for first, end in ((0, Q_COLS), (Q_COLS, QUERIES - HD), (QUERIES - HD, QUERIES)):
+        for first, end in ((0, Q_COLS), (Q_COLS, QUERIES - HD)):
             add_products(nc.vector, i, first, end)
             store_queries(i, first, end)
-            if first == 0:
-                store_keys(i)
+        add_products(nc.vector, i, QUERIES, ALL - shared_heads(i) * HD)
+        store_keys(i)
+        add_products(nc.vector, i, QUERIES - HD, QUERIES)
+        store_queries(i, QUERIES - HD, QUERIES)

from contextlib import ExitStack

import concourse.mybir as mybir
from concourse.masks import make_identity

F32 = mybir.dt.float32
BF16 = mybir.dt.bfloat16
U32 = mybir.dt.uint32
U8 = mybir.dt.uint8
FP8X4 = mybir.dt.float8_e4m3fn_x4
MULT = mybir.AluOpType.mult
ADD = mybir.AluOpType.add

P = 128
B, S, D = 2, 2048, 1024
HD = 128
HALF = HD // 2
Q_COLS, K_COLS, V_COLS = 512, 256, 256
QK_COLS = Q_COLS + K_COLS
K_PASS = 512
PASSES = D // K_PASS
PACK = 4
SLOTS = 2
BLOCK = P * SLOTS
N_BLOCKS = B * S // BLOCK
POS_BLOCKS = S // BLOCK
WORDS = D // 2
EARLY = 2
QUANTISED_AFTER = {0: (2, 3), 2: (4, 5), 4: (6, 7, 8), 7: (9, 10, 11, 12), 11: (13, 14, 15)}
TRANSPOSED_IN = {1: (4,), 2: (5,), 3: (6, 7), 4: (8,), 5: (9, 10), 6: (11,), 7: (12,), 8: (13,), 9: (14,), 10: (15,)}
TENSOR_ADDS_FROM = 10
SORTED_FROM = 6

FLOPS = 2 * B * S * D * (QK_COLS + V_COLS)


def tile_attention_pa_t_kernel(tc, x, cos, sin, Wq, Wk, Wv, out_0, out_1, out_2):
    nc = tc.nc
    x_blocks = x.rearrange("b (p n s) k -> b n p (s k)", n=POS_BLOCKS, s=SLOTS)
    q_blocks = out_0.rearrange("b (p n s) h d -> b n p (s h d)", n=POS_BLOCKS, s=SLOTS)
    k_blocks = out_1.rearrange("b (p n s) h d -> b n p (s h d)", n=POS_BLOCKS, s=SLOTS)
    v_blocks = out_2.rearrange("b (p n s) h d -> b n p (s h d)", n=POS_BLOCKS, s=SLOTS)
    cos_rows = cos.rearrange("(p n s) d -> p n (s d)", p=P, s=SLOTS)
    sin_rows = sin.rearrange("(p n s) d -> p n (s d)", p=P, s=SLOTS)

    with ExitStack() as ctx:
        keep = ctx.enter_context(tc.tile_pool(name="keep", bufs=1))
        x_pool = ctx.enter_context(tc.tile_pool(name="x_pool", bufs=N_BLOCKS))
        quant = ctx.enter_context(tc.tile_pool(name="quant", bufs=8))
        result = ctx.enter_context(tc.tile_pool(name="result", bufs=5))
        xt_psum = ctx.enter_context(tc.psum_pool(name="xt_psum", bufs=2))
        acc_psum = ctx.enter_context(tc.psum_pool(name="acc_psum", bufs=6))

        ident = keep.tile([P, P], F32)
        make_identity(nc, ident[:])

        ctx.enter_context(tc.manual_schedule())

        def weight_tiles(cols, name):
            raw = []
            grouped = keep.tile([P, PASSES, cols, PACK], BF16, name=name + "_grouped", align_bytes=64)
            codes = keep.tile([P, PASSES, cols], U32, name=name + "_codes", align_bytes=64)
            scales = keep.tile([P, PASSES, cols], U8, name=name + "_scales", align_bytes=64)
            return raw, grouped, codes, scales

        def load_weight(weight, w):
            cols = w.shape[1]
            for c in range(PASSES):
                if c * PACK * cols % (SLOTS * D) == 0:
                    raw = x_pool.tile([P, SLOTS * D], BF16, name="x_blk")
                first = c * PACK * cols % (SLOTS * D)
                part = raw[:, first : first + PACK * cols].rearrange("p (t n) -> p t n", t=PACK)
                weight[0].append(part)
                nc.sync.dma_start(
                    out=part, in_=w[c * K_PASS : (c + 1) * K_PASS, :].rearrange("(p t) n -> p t n", t=PACK)
                )

        x_tiles = []

        def load_x():
            i = len(x_tiles)
            x_blk = x_pool.tile([P, SLOTS * D], BF16)
            nc.sync.dma_start(out=x_blk[:], in_=x_blocks[i // POS_BLOCKS, i % POS_BLOCKS])
            x_tiles.append(x_blk)

        sin_raw = keep.tile([P, POS_BLOCKS, SLOTS, HD], BF16)
        tables = keep.tile([P, POS_BLOCKS, 2, SLOTS, HD], BF16)

        def load_tables(blocks):
            nc.sync.dma_start(
                out=tables[:, blocks, 0, :, :].rearrange("p n s d -> p n (s d)"), in_=cos_rows[:, blocks, :]
            )
            nc.sync.dma_start(
                out=sin_raw[:, blocks, :, :].rearrange("p n s d -> p n (s d)"), in_=sin_rows[:, blocks, :]
            )

        wq, wk, wv = weight_tiles(Q_COLS, "wq"), weight_tiles(K_COLS, "wk"), weight_tiles(V_COLS, "wv")
        x_first = x_pool.tile([P, SLOTS * D], BF16, name="x_blk")
        nc.sync.dma_start(out=x_first[:, 0:D], in_=x_blocks[0, 0][:, 0:D])
        load_weight(wk, Wk)
        nc.sync.dma_start(out=x_first[:, D : SLOTS * D], in_=x_blocks[0, 0][:, D : SLOTS * D])
        x_tiles.append(x_first)
        load_tables(slice(0, EARLY))
        load_x()
        load_weight(wq, Wq)
        load_x()
        load_weight(wv, Wv)
        load_x()
        load_tables(slice(EARLY, POS_BLOCKS))
        while len(x_tiles) < N_BLOCKS:
            load_x()

        def regroup_weight(copy, weight, c, cols):
            copy(
                out=weight[1][:, c, cols, :].rearrange("p (n i) t -> p n t i", i=4),
                in_=weight[0][c][:, :, cols].rearrange("p t (n i) -> p n t i", i=4),
            )

        def quantise_weight(weight, passes):
            grouped, codes, scales = weight[1:]
            nc.vector.quantize_mx(
                out=codes[:, passes, :].rearrange("p c n -> p (c n)").bitcast(FP8X4),
                scales=scales[:, passes, :].rearrange("p c n -> p (c n)"),
                in_=grouped[:, passes, :, :].rearrange("p c n t -> p (c n t)"),
            )

        grouped_of = {}
        codes_of = {}

        sorted_of = {}

        def sort_words(i):
            x_sorted = quant.tile([P, SLOTS * WORDS], F32, bufs=4)
            nc.scalar.copy(
                out=x_sorted[:].rearrange("p (g u r) -> p g u r", u=2, r=P),
                in_=x_tiles[i][:].bitcast(F32).rearrange("p (g r u) -> p g u r", u=2, r=P),
            )
            sorted_of[i] = x_sorted

        def transpose_block(i):
            x_words = x_tiles[i][:].bitcast(F32)
            grouped = quant.tile([P, SLOTS * D], BF16, align_bytes=64, bufs=6)
            grouped_words = grouped[:].bitcast(F32)
            for s in range(SLOTS):
                xt = xt_psum.tile([P, WORDS], F32)
                for j in range(WORDS // P):
                    c, u = divmod(j, 2)
                    first = s * WORDS + c * 2 * P
                    if i < SORTED_FROM:
                        words = x_words[:, first + u : first + 2 * P : 2]
                    else:
                        words = sorted_of[i][:, first + u * P : first + (u + 1) * P]
                    nc.tensor.transpose(xt[:, j * P : (j + 1) * P], words, ident[:])
                nc.scalar.copy(
                    out=grouped_words[:, s * WORDS : (s + 1) * WORDS].rearrange(
                        "p (c r u) -> p c r u", c=PASSES, u=2
                    ),
                    in_=xt[:].rearrange("p (c u r) -> p c r u", c=PASSES, u=2),
                )
            x_codes = quant.tile([P, SLOTS * PASSES * P], U32, align_bytes=64)
            x_scales = quant.tile([P, SLOTS * PASSES * P], U8, align_bytes=64)
            grouped_of[i] = grouped
            codes_of[i] = (x_codes, x_scales)

        def quantise_block(i, first_slot, slots):
            x_codes, x_scales = codes_of[i]
            first, end = first_slot * PASSES * P, (first_slot + slots) * PASSES * P
            nc.vector.quantize_mx(
                out=x_codes[:, first:end].bitcast(FP8X4),
                scales=x_scales[:, first:end],
                in_=grouped_of[i][:, first * PACK : end * PACK],
            )

        def project(bank_cols, i, s, weight):
            x_codes, x_scales = codes_of[i]
            for c in range(PASSES):
                tokens = slice((s * PASSES + c) * P, (s * PASSES + c + 1) * P)
                nc.tensor.matmul_mx(
                    out=bank_cols,
                    lhsT=x_codes[:, tokens].bitcast(FP8X4),
                    lhsT_scale=x_scales[:, tokens],
                    rhs=weight[2][:, c, :].bitcast(FP8X4),
                    rhs_scale=weight[3][:, c, :],
                    start=(c == 0),
                    stop=(c == PASSES - 1),
                )

        def project_both(i, weight, cols):
            bank = acc_psum.tile([P, SLOTS * cols], F32, tag="acc")
            for s in range(SLOTS):
                project(bank[:, s * cols : (s + 1) * cols], i, s, weight)
            return bank

        def project_queries(i):
            banks = []
            for s in range(SLOTS):
                bank = acc_psum.tile([P, Q_COLS], F32, tag="acc")
                project(bank[:], i, s, wq)
                banks.append(bank)
            return banks

        both_of = {}

        def rope_products(bank, i, first_slot, slots, first_col):
            cols = bank.shape[1]
            shape = [P, 2, slots, cols // (slots * HD), HD]
            nc.vector.tensor_tensor(
                out=both_of[i][:, :, first_col : first_col + cols].rearrange("p w (s h d) -> p w s h d", s=slots, d=HD),
                in0=bank.rearrange("p (s h d) -> p s h d", s=slots, d=HD).unsqueeze(1).to_broadcast(shape),
                in1=tables[:, i % POS_BLOCKS, :, first_slot : first_slot + slots, :].unsqueeze(3).to_broadcast(shape),
                op=MULT,
            )

        def add_products(engine, i, first, end):
            by_cos = both_of[i][:, 0, first:end].rearrange("p (g t j) -> p g t j", t=2, j=HALF)
            by_sin = both_of[i][:, 1, first:end].rearrange("p (g t j) -> p g t j", t=2, j=HALF)
            engine.tensor_tensor(out=by_cos, in0=by_cos, in1=by_sin[:, :, ::-1, :], op=ADD)

        def build_tables(copy, negate, blocks):
            copy(out=tables[:, blocks, 1, :, 0:HALF], in_=sin_raw[:, blocks, :, HALF:HD])
            negate(tables[:, blocks, 1, :, HALF:HD], sin_raw[:, blocks, :, 0:HALF])

        def vector_negate(out, in_):
            nc.vector.tensor_scalar_mul(out=out, in0=in_, scalar1=-1.0)

        def scalar_negate(out, in_):
            nc.scalar.mul(out, in_, -1.0)

        QUERIES = SLOTS * Q_COLS
        ALL = SLOTS * QK_COLS

        def store_values(i, bank):
            values = result.tile([P, SLOTS * V_COLS], F32, bufs=4)
            nc.scalar.copy(out=values[:], in_=bank[:])
            nc.sync.dma_start(out=v_blocks[i // POS_BLOCKS, i % POS_BLOCKS], in_=values[:])

        def store_keys(i):
            nc.sync.dma_start(out=k_blocks[i // POS_BLOCKS, i % POS_BLOCKS], in_=both_of[i][:, 0, QUERIES:ALL])

        def store_queries(i, first, end):
            nc.sync.dma_start(
                out=q_blocks[i // POS_BLOCKS, i % POS_BLOCKS][:, first:end], in_=both_of[i][:, 0, first:end]
            )

        def shared_heads(i):
            if i == N_BLOCKS - 1:
                return SLOTS * K_COLS // HD - 1
            return 0 if i < 2 else 2 if i >= TENSOR_ADDS_FROM else 2 - i % 2

        def vector_adds(i):
            if shared_heads(i):
                add_products(nc.vector, i, ALL - shared_heads(i) * HD, ALL)

        def tensor_adds(i):
            cols = shared_heads(i) * HD
            bank = acc_psum.tile([P, cols], F32, tag="acc")
            sums = bank[:].rearrange("p (g t j) -> p g t j", t=2, j=HALF)
            by_cos = both_of[i][:, 0, ALL - cols : ALL].rearrange("p (g t j) -> p g t j", t=2, j=HALF)
            by_sin = both_of[i][:, 1, ALL - cols : ALL].rearrange("p (g t j) -> p g t j", t=2, j=HALF)
            for t in range(2):
                nc.tensor.matmul(out=sums[:, :, t, :], lhsT=ident[:], rhs=by_cos[:, :, t, :], start=True, stop=False)
                nc.tensor.matmul(out=sums[:, :, t, :], lhsT=ident[:], rhs=by_sin[:, :, 1 - t, :], start=False, stop=True)
            nc.scalar.copy(out=both_of[i][:, 0, ALL - cols : ALL], in_=bank[:])

        def gpsimd_adds(i):
            add_products(nc.gpsimd, i, 0, QUERIES if i < 2 else ALL - shared_heads(i) * HD)

        def new_block(i):
            both_of[i] = result.tile([P, 2, ALL], F32, name="both")

        k_banks = {}

        def keys(i):
            rope_products(k_banks[i][:], i, 0, SLOTS, QUERIES)

        def queries(i, banks, s, first, end):
            rope_products(banks[s][:, first:end], i, s, 1, s * Q_COLS + first)

        zeros = keep.tile([P, Q_COLS], BF16)
        nc.vector.memset(zeros[:], 0.0)

        def warm_up(products):
            bank = acc_psum.tile([P, Q_COLS], F32, tag="acc")
            for j in range(products):
                nc.tensor.matmul(out=bank[:], lhsT=zeros[:, 0:P], rhs=zeros[:], start=True, stop=True)

        new_block(0)
        warm_up(4)
        transpose_block(0)
        warm_up(2)
        for c in range(PASSES):
            regroup_weight(nc.vector.tensor_copy, wk, c, slice(0, K_COLS))
        quantise_block(0, 0, 1)
        quantise_weight(wk, slice(0, PASSES))
        build_tables(nc.vector.tensor_copy, vector_negate, slice(0, EARLY))
        quantise_block(0, 1, 1)
        first_half, second_half = slice(0, Q_COLS // 2), slice(Q_COLS // 2, Q_COLS)
        new_block(1)
        for s in range(SLOTS):
            bank = acc_psum.tile([P, K_COLS], F32, tag="acc")
            project(bank[:], 0, s, wk)
            rope_products(bank[:], 0, s, 1, QUERIES + s * K_COLS)
            if s == 0:
                transpose_block(1)
                regroup_weight(nc.vector.tensor_copy, wq, 0, first_half)
        warm_up(6)
        for c in range(PASSES):
            regroup_weight(nc.scalar.copy, wq, c, second_half)
        quantise_block(1, 0, SLOTS)
        regroup_weight(nc.vector.tensor_copy, wq, 1, first_half)
        k_banks[1] = project_both(1, wk, K_COLS)
        regroup_weight(nc.scalar.copy, wv, 0, slice(0, V_COLS))
        transpose_block(2)
        regroup_weight(nc.scalar.copy, wv, 1, slice(0, V_COLS))
        for c in range(PASSES):
            quantise_weight(wq, slice(c, c + 1))
        keys(1)
        for j in range(2):
            add_products(nc.gpsimd, j, QUERIES, ALL)

        SPLIT = Q_COLS - HD
        added = 0
        stored = 0
        projected = 0
        for i in range(N_BLOCKS):
            last = i == N_BLOCKS - 1
            if i > 1:
                new_block(i)
                keys(i)
            q_banks = project_queries(i)
            queries(i, q_banks, 0, 0, Q_COLS)
            if i == 0:
                transpose_block(3)
                build_tables(nc.scalar.copy, scalar_negate, slice(EARLY, POS_BLOCKS))
            for j in TRANSPOSED_IN.get(i, ()):
                transpose_block(j)
            for j in TRANSPOSED_IN.get(i + 2, ()):
                if j >= SORTED_FROM:
                    sort_words(j)
            if 0 < i < N_BLOCKS - 1:
                k_banks[i + 1] = project_both(i + 1, wk, K_COLS)
            if i > TENSOR_ADDS_FROM:
                tensor_adds(i - 1)
            while projected < min(N_BLOCKS, i - 1 + sum(2 < j <= i for j in QUANTISED_AFTER)):
                store_values(projected, project_both(projected, wv, V_COLS))
                projected += 1
            if last:
                queries(i, q_banks, 1, 0, Q_COLS)
            elif i in QUANTISED_AFTER:
                queries(i, q_banks, 1, 0, SPLIT)
                if i == 0:
                    quantise_weight(wv, slice(0, PASSES))
                for j in range(added, min(i + 1, TENSOR_ADDS_FROM)):
                    vector_adds(j)
                    added = j + 1
                for j in QUANTISED_AFTER[i]:
                    quantise_block(j, 0, SLOTS)
                queries(i, q_banks, 1, SPLIT, Q_COLS)
                gpsimd_adds(i)
            else:
                queries(i, q_banks, 1, 0, Q_COLS)
                gpsimd_adds(i)
            if i > TENSOR_ADDS_FROM:
                added = i
            if 0 < i and not last:
                store_queries(i - 1, 0, QUERIES)
                for j in range(stored, min(added, i)):
                    store_keys(j)
                    stored = j + 1
        i = N_BLOCKS - 1
        tensor_adds(i)
        store_queries(i - 1, 0, QUERIES)
        store_keys(i - 1)
        for first, end in ((0, Q_COLS), (Q_COLS, QUERIES - HD)):
            add_products(nc.vector, i, first, end)
            store_queries(i, first, end)
        add_products(nc.vector, i, QUERIES, ALL - shared_heads(i) * HD)
        store_keys(i)
        add_products(nc.vector, i, QUERIES - HD, QUERIES)
        store_queries(i, QUERIES - HD, QUERIES)
